import numpy as np
import ml_dtypes


def mxq(x, axis, fmt="e4m3"):
    dtype, down = {"e4m3": (ml_dtypes.float8_e4m3fn, 7), "e5m2": (ml_dtypes.float8_e5m2, 14)}[fmt]
    v = np.moveaxis(np.asarray(x, np.float32).astype(ml_dtypes.bfloat16).astype(np.float64), axis, -1)
    blocks = v.reshape(v.shape[:-1] + (-1, 32))
    amax = np.abs(blocks).max(-1, keepdims=True)
    byte = np.maximum(np.where(amax > 0, np.frexp(amax)[1] - 1 + 127, 0) - down, 1)
    scale = np.exp2(byte - 127.0)
    codes = (blocks / scale).astype(np.float32).astype(dtype).astype(np.float64)
    return np.moveaxis((codes * scale).reshape(v.shape), -1, axis)


WIDE = False


def mx_kscale(k):
    if not WIDE:
        return np.ones(k)
    levels = np.array([10, -10, 5, -5, 0])
    if k % 512:
        return np.exp2(np.random.permutation(np.resize(levels, k // 32))).repeat(32)
    a = np.empty((k // 512, 16))
    for p in range(k // 512):
        a[p, :8] = np.random.permutation(np.resize(levels, 8))
        for g in range(8):
            far = levels[np.abs(levels - a[p, g]) >= 10]
            a[p, g + 8] = far[np.random.randint(len(far))]
    return np.exp2(a.ravel()).repeat(32)


BF16 = ml_dtypes.bfloat16


def bf(x):
    return np.asarray(x, np.float32).astype(BF16)


def f64(x):
    return np.asarray(x).astype(np.float64)


B, D, H, F, K = 2048, 1024, 1024, 1024, 128
EPS_LN = 1e-5


def silu(v):
    return v / (1.0 + np.exp(-v))


def setup_inputs():
    s = mx_kscale(D)
    return {"x": bf(np.random.standard_normal((B, D)) * s),
            "W1": bf(np.random.standard_normal((D, H)) / np.sqrt(D) / s[:, None]),
            "b1": bf(0.2 * np.random.standard_normal(H)),
            "g": bf(1.0 + 0.1 * np.random.standard_normal(H)),
            "beta": bf(0.1 * np.random.standard_normal(H))}


def core(x, W1, b1, g, beta):
    h = silu((mxq(f64(x), 1, "e4m3") @ mxq(f64(W1), 0, "e4m3")) + f64(b1))
    mu = h.mean(-1, keepdims=True)
    var = ((h - mu) ** 2).mean(-1, keepdims=True)
    return (h - mu) / np.sqrt(var + EPS_LN) * f64(g) + f64(beta)


def e4m3fn_bytes(y):
    return np.clip(np.asarray(y, np.float64), -448.0, 448.0).astype(np.float32).astype(ml_dtypes.float8_e4m3fn).view(np.uint8)


def reference(x, W1, b1, g, beta):
    out = core(x, W1, b1, g, beta)
    s = np.max(np.abs(out)) / 448.0
    return out, e4m3fn_bytes(out / s)

@@ -1,0 +1,292 @@
+from contextlib import ExitStack
+
+import concourse.mybir as mybir
+from concourse.masks import make_identity
+
+B, D, H = 2048, 1024, 1024
+EPS_LN = 1e-5
+FLOPS = 2 * B * D * H
+
+F32 = mybir.dt.float32
+BF16 = mybir.dt.bfloat16
+U32 = mybir.dt.uint32
+U8 = mybir.dt.uint8
+FP8X4 = mybir.dt.float8_e4m3fn_x4
+FP8 = mybir.dt.float8_e4m3fn
+ALU = mybir.AluOpType
+ACT = mybir.ActivationFunctionType
+AX = mybir.AxisListType
+
+P = 128
+NT = B // P
+GT = 2
+NG = NT // GT
+NTOK = GT * P
+KP = D // 512
+NJ = H // P
+HB = 512
+W_V_COLS = 256
+CAST_V_COLS = 1376
+
+
+def tile_evidentialhead_pa_kernel(tc, x, W1, b1, g, beta, out_0, out_1):
+    nc = tc.nc
+    x_v = x.rearrange("(p i) k -> p i k", i=NT)
+    o0_v = out_0.rearrange("(p i) c -> p i c", i=NT)
+    o1_v = out_1.rearrange("(p i) c -> p (i c)", i=NT)
+
+    with ExitStack() as ctx:
+        const = ctx.enter_context(tc.tile_pool(name="const", bufs=1))
+        xraw = ctx.enter_context(tc.tile_pool(name="xraw", bufs=NG))
+        wtmp = ctx.enter_context(tc.tile_pool(name="wtmp", bufs=4))
+        xprep = ctx.enter_context(tc.tile_pool(name="xprep", bufs=2))
+        hpool = ctx.enter_context(tc.tile_pool(name="hpool", bufs=2))
+        work = ctx.enter_context(tc.tile_pool(name="work", bufs=2))
+        stat = ctx.enter_context(tc.tile_pool(name="stat", bufs=4))
+        opool = ctx.enter_context(tc.tile_pool(name="opool", bufs=NG))
+        psum = ctx.enter_context(tc.psum_pool(name="psum", bufs=2))
+        ctx.enter_context(tc.manual_schedule())
+
+        warm = const.tile([P, 2], F32, name="warm")
+        nc.vector.memset(warm[:], 0.0)
+        nc.scalar.activation(out=warm[:, 1:2], in_=warm[:, 0:1], func=ACT.Silu)
+        zero = const.tile([P, 1], F32, name="zero")
+        nc.vector.memset(zero[:], 0.0)
+        mhalf = const.tile([P, 1], F32, name="mhalf")
+        nc.vector.memset(mhalf[:], -0.5)
+        ident = const.tile([P, P], F32, name="ident")
+        make_identity(nc, ident[:])
+
+        b1_bf = const.tile([P, NJ], BF16, name="b1_bf")
+        with nc.allow_non_contiguous_dma(reason="one bias value to a partition"):
+            nc.scalar.dma_start(out=b1_bf[:], in_=b1.rearrange("(c p) -> p c", p=P))
+
+        xr = []
+        wr = []
+
+        def load_x(s):
+            t = xraw.tile([P, GT, D], BF16, name="xr", tag="xr")
+            nc.sync.dma_start(out=t[:], in_=x_v[:, GT * s : GT * (s + 1), :])
+            xr.append(t)
+
+        chunks = [(0, 0), (1, 0), (0, 1), (1, 1)]
+        load_x(0)
+        for kp, hf in chunks:
+            t = wtmp.tile([P, 4, HB], BF16, name="wr", tag="wr")
+            nc.sync.dma_start(
+                out=t[:],
+                in_=W1[512 * kp : 512 * (kp + 1), HB * hf : HB * (hf + 1)].rearrange("(p j) w -> p j w", j=4),
+            )
+            wr.append(t)
+        load_x(1)
+        g_bc = const.tile([P, H], BF16, name="g_bc")
+        nc.sync.dma_start(out=g_bc[:], in_=g.partition_broadcast(P))
+        beta_bc = const.tile([P, H], BF16, name="beta_bc")
+        nc.sync.dma_start(out=beta_bc[:], in_=beta.partition_broadcast(P))
+        for s in range(2, NG):
+            load_x(s)
+
+        b1f = const.tile([P, NJ], F32, name="b1f")
+        nc.vector.tensor_copy(out=b1f[:], in_=b1_bf[:])
+        am = const.tile([P, NT], F32, name="am")
+
+        wc = {}
+        ws = {}
+        xt_ps = {}
+        xg = {}
+        xc = {}
+        xs = {}
+        hs = {}
+        ht_ps = {}
+        sp = {}
+        gs = {}
+        tt = {}
+        ob = {}
+
+        def w_copy(c):
+            t = wtmp.tile([P, HB, 4], BF16, name="wg", tag="wg", align_bytes=64)
+            nc.vector.tensor_copy(out=t[:, 0:W_V_COLS, :], in_=wr[c][:, :, 0:W_V_COLS].rearrange("p j w -> p w j"))
+            nc.scalar.copy(out=t[:, W_V_COLS:HB, :], in_=wr[c][:, :, W_V_COLS:HB].rearrange("p j w -> p w j"))
+            return t
+
+        def w_quant(c, t):
+            codes = const.tile([P, HB], U32, name="wc%d" % c, align_bytes=64)
+            scales = const.tile([P, HB], U8, name="ws%d" % c, align_bytes=64)
+            nc.vector.quantize_mx(out=codes[:].bitcast(FP8X4), scales=scales[:], in_=t[:].rearrange("p w j -> p (w j)"))
+            wc[chunks[c]] = codes
+            ws[chunks[c]] = scales
+
+        def w_prep():
+            t0 = w_copy(0)
+            t1 = w_copy(1)
+            w_quant(0, t0)
+            t2 = w_copy(2)
+            w_quant(1, t1)
+            t3 = w_copy(3)
+            w_quant(2, t2)
+            w_quant(3, t3)
+
+        def x_transpose(s):
+            xg[s] = xprep.tile([P, KP, NTOK, 4], BF16, name="xg", tag="xg", align_bytes=64)
+            for tl in range(GT):
+                ps = psum.tile([P, KP, 2, P], F32, name="xt", tag="xt")
+                words = xr[s][:, tl, :].bitcast(F32)
+                for kp in range(KP):
+                    for u in range(2):
+                        nc.tensor.transpose(ps[:, kp, u, :], words[:, 256 * kp + u : 256 * (kp + 1) : 2], ident[:])
+                xt_ps[(s, tl)] = ps
+
+        def x_evac(s, tl, on_vector):
+            dst = xg[s][:].rearrange("p k r e -> p (k r e)").bitcast(F32).rearrange("p (k r u) -> p k r u", k=KP, u=2)
+            dst = dst[:, :, tl * P : (tl + 1) * P, :]
+            src = xt_ps[(s, tl)][:].rearrange("p k u r -> p k r u")
+            if on_vector:
+                nc.vector.tensor_copy(out=dst, in_=src)
+            else:
+                nc.scalar.copy(out=dst, in_=src)
+
+        def x_quant(s):
+            xc[s] = xprep.tile([P, KP * NTOK], U32, name="xc", tag="xc", align_bytes=64)
+            xs[s] = xprep.tile([P, KP * NTOK], U8, name="xs", tag="xs", align_bytes=64)
+            nc.vector.quantize_mx(
+                out=xc[s][:].bitcast(FP8X4), scales=xs[s][:], in_=xg[s][:].rearrange("p k r e -> p (k r e)")
+            )
+
+        def mm(s, jp):
+            if jp == 0:
+                hs[s] = hpool.tile([P, NJ, NTOK], F32, name="h", tag="h")
+            acc = psum.tile([P, 2, NTOK], F32, name="acc", tag="acc")
+            for jj in range(2):
+                j = 2 * jp + jj
+                cols = slice((j % 4) * P, (j % 4 + 1) * P)
+                for kp in range(KP):
+                    toks = slice(kp * NTOK, (kp + 1) * NTOK)
+                    nc.tensor.matmul_mx(
+                        out=acc[:, jj, :],
+                        lhsT=wc[(kp, j // 4)][:, cols].bitcast(FP8X4),
+                        lhsT_scale=ws[(kp, j // 4)][:, cols],
+                        rhs=xc[s][:, toks].bitcast(FP8X4),
+                        rhs_scale=xs[s][:, toks],
+                        start=(kp == 0),
+                        stop=(kp == KP - 1),
+                    )
+            for jj in range(2):
+                j = 2 * jp + jj
+                nc.scalar.activation(out=hs[s][:, j, :], in_=acc[:, jj, :], func=ACT.Silu, bias=b1f[:, j : j + 1], scale=1.0)
+
+        def h_transpose(i):
+            s, tl = i // GT, i % GT
+            banks = []
+            for half in range(2):
+                ps = psum.tile([P, HB], F32, name="ht%d" % half, tag="ht%d" % half)
+                for q in range(4):
+                    nc.tensor.transpose(ps[:, q * P : (q + 1) * P], hs[s][:, 4 * half + q, tl * P : (tl + 1) * P], ident[:])
+                banks.append(ps)
+            ht_ps[i] = banks
+
+        def mean(i):
+            sp[i] = stat.tile([P, 4], F32, name="sp", tag="sp")
+            gs[i] = stat.tile([P, 4], F32, name="gs", tag="gs")
+            for half in range(2):
+                junk = stat.tile([P, HB], BF16, name="junk", tag="junk")
+                nc.scalar.activation(
+                    out=junk[:], in_=ht_ps[i][half][:], func=ACT.Copy, scale=-1.0 / H, accum_out=sp[i][:, half : half + 1]
+                )
+            nc.gpsimd.tensor_tensor(out=gs[i][:, 0:1], in0=sp[i][:, 0:1], in1=sp[i][:, 1:2], op=ALU.add)
+
+        def rstd(i):
+            for half in range(2):
+                junk = stat.tile([P, HB], BF16, name="junk", tag="junk")
+                nc.scalar.activation(
+                    out=junk[:],
+                    in_=ht_ps[i][half][:],
+                    func=ACT.Square,
+                    bias=gs[i][:, 0:1],
+                    scale=1.0,
+                    accum_out=sp[i][:, 2 + half : 3 + half],
+                )
+            nc.gpsimd.tensor_scalar(
+                out=gs[i][:, 1:2], in0=sp[i][:, 2:3], scalar1=sp[i][:, 3:4], scalar2=1.0 / H, op0=ALU.add, op1=ALU.mult
+            )
+            nc.gpsimd.tensor_scalar(out=gs[i][:, 2:3], in0=gs[i][:, 1:2], scalar1=1.0, scalar2=EPS_LN, op0=ALU.mult, op1=ALU.add)
+            nc.gpsimd.tensor_tensor(out=gs[i][:, 3:4], in0=gs[i][:, 2:3], in1=mhalf[:], op=ALU.pow)
+
+        def v1(i):
+            tt[i] = work.tile([P, H], F32, name="t", tag="t")
+            for half in range(2):
+                cols = slice(half * HB, (half + 1) * HB)
+                nc.vector.scalar_tensor_tensor(
+                    out=tt[i][:, cols], in0=ht_ps[i][half][:], scalar=gs[i][:, 0:1], in1=g_bc[:, cols], op0=ALU.add, op1=ALU.mult
+                )
+
+        def v2(i):
+            s, tl = i // GT, i % GT
+            if tl == 0:
+                ob[s] = opool.tile([P, GT, H], F32, name="o", tag="o")
+            nc.vector.scalar_tensor_tensor(
+                out=ob[s][:, tl, :], in0=tt[i][:], scalar=gs[i][:, 3:4], in1=beta_bc[:], op0=ALU.mult, op1=ALU.add
+            )
+
+        def v3(s):
+            nc.vector.tensor_reduce(
+                out=am[:, GT * s : GT * (s + 1)], in_=ob[s][:], axis=AX.X, op=ALU.max, apply_absolute_value=True
+            )
+            nc.sync.dma_start(out=o0_v[:, GT * s : GT * (s + 1), :], in_=ob[s][:])
+
+        for s in range(-3, NG):
+            a, b = GT * s, GT * s + 1
+            if s >= 0:
+                v1(a)
+                v1(b)
+            if 0 <= s + 1 < NG:
+                h_transpose(a + GT)
+                h_transpose(b + GT)
+            if 0 <= s + 2 < NG:
+                x_evac(s + 2, 1, True)
+                x_quant(s + 2)
+            if s == -2:
+                w_prep()
+            if 0 <= s + 1 < NG:
+                mean(a + GT)
+                mean(b + GT)
+            if 0 <= s + 2 < NG:
+                mm(s + 2, 0)
+                mm(s + 2, 1)
+            if 0 <= s + 3 < NG:
+                x_transpose(s + 3)
+                x_evac(s + 3, 0, False)
+            if 0 <= s + 1 < NG:
+                rstd(a + GT)
+                rstd(b + GT)
+            if 0 <= s + 2 < NG:
+                mm(s + 2, 2)
+                mm(s + 2, 3)
+            if s >= 0:
+                v2(a)
+                v2(b)
+                v3(s)
+
+        gm = const.tile([P, 4], F32, name="gm")
+        nc.vector.tensor_reduce(out=gm[:, 0:1], in_=am[:], axis=AX.X, op=ALU.max)
+        spread = psum.tile([P, P], F32, name="spread", tag="xt")
+        nc.tensor.transpose(spread[:], gm[:, 0:1].to_broadcast([P, P]), ident[:])
+        nc.vector.tensor_reduce(out=gm[:, 1:2], in_=spread[:], axis=AX.X, op=ALU.max)
+        nc.vector.reciprocal(out=gm[:, 2:3], in_=gm[:, 1:2])
+        nc.vector.tensor_scalar(out=gm[:, 3:4], in0=gm[:, 2:3], scalar1=448.0, scalar2=None, op0=ALU.mult)
+        factor = gm[:, 3:4]
+
+        for s in range(NG):
+            flat = ob[s][:].rearrange("p a c -> p (a c)")
+            f8 = opool.tile([P, GT * H], FP8, name="f8", tag="f8")
+            nc.vector.tensor_scalar(
+                out=f8[:, 0:CAST_V_COLS], in0=flat[:, 0:CAST_V_COLS], scalar1=factor, scalar2=None, op0=ALU.mult, saturate=False
+            )
+            nc.scalar.activation(
+                out=f8[:, CAST_V_COLS:],
+                in_=flat[:, CAST_V_COLS:],
+                func=ACT.Identity,
+                scale=factor,
+                bias=zero[:, 0:1],
+                saturate=False,
+            )
+            nc.sync.dma_start(out=o1_v[:, GT * H * s : GT * H * (s + 1)], in_=f8[:].bitcast(U8))

@@ -98,6 +98,7 @@ def tile_evidentialhead_pa_kernel(tc, x, W1, b1, g, beta, out_0, out_1):
         xs = {}
         hs = {}
         ht_ps = {}
+        fold_ps = {}
         sp = {}
         gs = {}
         tt = {}
@@ -116,25 +117,15 @@ def tile_evidentialhead_pa_kernel(tc, x, W1, b1, g, beta, out_0, out_1):
             wc[chunks[c]] = codes
             ws[chunks[c]] = scales
 
-        def w_prep():
-            t0 = w_copy(0)
-            t1 = w_copy(1)
-            w_quant(0, t0)
-            t2 = w_copy(2)
-            w_quant(1, t1)
-            t3 = w_copy(3)
-            w_quant(2, t2)
-            w_quant(3, t3)
-
-        def x_transpose(s):
-            xg[s] = xprep.tile([P, KP, NTOK, 4], BF16, name="xg", tag="xg", align_bytes=64)
-            for tl in range(GT):
-                ps = psum.tile([P, KP, 2, P], F32, name="xt", tag="xt")
-                words = xr[s][:, tl, :].bitcast(F32)
-                for kp in range(KP):
-                    for u in range(2):
-                        nc.tensor.transpose(ps[:, kp, u, :], words[:, 256 * kp + u : 256 * (kp + 1) : 2], ident[:])
-                xt_ps[(s, tl)] = ps
+        def x_transpose(s, tl):
+            if tl == 0:
+                xg[s] = xprep.tile([P, KP, NTOK, 4], BF16, name="xg", tag="xg", align_bytes=64)
+            ps = psum.tile([P, KP, 2, P], F32, name="xt", tag="xt", bufs=1)
+            words = xr[s][:, tl, :].bitcast(F32)
+            for kp in range(KP):
+                for u in range(2):
+                    nc.tensor.transpose(ps[:, kp, u, :], words[:, 256 * kp + u : 256 * (kp + 1) : 2], ident[:])
+            xt_ps[(s, tl)] = ps
 
         def x_evac(s, tl, on_vector):
             dst = xg[s][:].rearrange("p k r e -> p (k r e)").bitcast(F32).rearrange("p (k r u) -> p k r u", k=KP, u=2)
@@ -176,6 +167,17 @@ def tile_evidentialhead_pa_kernel(tc, x, W1, b1, g, beta, out_0, out_1):
 
         def h_transpose(i):
             s, tl = i // GT, i % GT
+            fold = psum.tile([P, P], F32, name="fold", tag="mu", bufs=1)
+            for j in range(NJ):
+                nc.tensor.matmul(
+                    out=fold[:],
+                    lhsT=hs[s][:, j, tl * P : (tl + 1) * P],
+                    rhs=ident[:],
+                    is_transpose=True,
+                    start=(j == 0),
+                    stop=(j == NJ - 1),
+                )
+            fold_ps[i] = fold
             banks = []
             for half in range(2):
                 ps = psum.tile([P, HB], F32, name="ht%d" % half, tag="ht%d" % half)
@@ -187,12 +189,8 @@ def tile_evidentialhead_pa_kernel(tc, x, W1, b1, g, beta, out_0, out_1):
         def mean(i):
             sp[i] = stat.tile([P, 4], F32, name="sp", tag="sp")
             gs[i] = stat.tile([P, 4], F32, name="gs", tag="gs")
-            for half in range(2):
-                junk = stat.tile([P, HB], BF16, name="junk", tag="junk")
-                nc.scalar.activation(
-                    out=junk[:], in_=ht_ps[i][half][:], func=ACT.Copy, scale=-1.0 / H, accum_out=sp[i][:, half : half + 1]
-                )
-            nc.gpsimd.tensor_tensor(out=gs[i][:, 0:1], in0=sp[i][:, 0:1], in1=sp[i][:, 1:2], op=ALU.add)
+            junk = stat.tile([P, HB], BF16, name="junk", tag="junk")
+            nc.scalar.activation(out=junk[:, 0:P], in_=fold_ps[i][:], func=ACT.Copy, scale=-1.0 / H, accum_out=gs[i][:, 0:1])
 
         def rstd(i):
             for half in range(2):
@@ -226,53 +224,79 @@ def tile_evidentialhead_pa_kernel(tc, x, W1, b1, g, beta, out_0, out_1):
             nc.vector.scalar_tensor_tensor(
                 out=ob[s][:, tl, :], in0=tt[i][:], scalar=gs[i][:, 3:4], in1=beta_bc[:], op0=ALU.mult, op1=ALU.add
             )
+            if tl == GT - 1:
+                nc.sync.dma_start(out=o0_v[:, GT * s : GT * (s + 1), :], in_=ob[s][:])
 
-        def v3(s):
+        def v3(i):
+            s, tl = i // GT, i % GT
             nc.vector.tensor_reduce(
-                out=am[:, GT * s : GT * (s + 1)], in_=ob[s][:], axis=AX.X, op=ALU.max, apply_absolute_value=True
+                out=am[:, i : i + 1], in_=ob[s][:, tl, :], axis=AX.X, op=ALU.max, apply_absolute_value=True
             )
-            nc.sync.dma_start(out=o0_v[:, GT * s : GT * (s + 1), :], in_=ob[s][:])
 
-        for s in range(-3, NG):
+        x_transpose(0, 0)
+        x_evac(0, 0, False)
+        t0 = w_copy(0)
+        x_transpose(0, 1)
+        x_evac(0, 1, False)
+        t1 = w_copy(1)
+        w_quant(0, t0)
+        x_quant(0)
+        t2 = w_copy(2)
+        w_quant(1, t1)
+        t3 = w_copy(3)
+        w_quant(2, t2)
+        w_quant(3, t3)
+        for s in range(-1, NG):
             a, b = GT * s, GT * s + 1
             if s >= 0:
                 v1(a)
-                v1(b)
-            if 0 <= s + 1 < NG:
-                h_transpose(a + GT)
-                h_transpose(b + GT)
-            if 0 <= s + 2 < NG:
-                x_evac(s + 2, 1, True)
-                x_quant(s + 2)
-            if s == -2:
-                w_prep()
-            if 0 <= s + 1 < NG:
-                mean(a + GT)
-                mean(b + GT)
-            if 0 <= s + 2 < NG:
-                mm(s + 2, 0)
-                mm(s + 2, 1)
-            if 0 <= s + 3 < NG:
-                x_transpose(s + 3)
-                x_evac(s + 3, 0, False)
-            if 0 <= s + 1 < NG:
-                rstd(a + GT)
-                rstd(b + GT)
-            if 0 <= s + 2 < NG:
-                mm(s + 2, 2)
-                mm(s + 2, 3)
+            if 0 < s + 1 < NG:
+                x_quant(s + 1)
+            if s == -1:
+                mm(0, 0)
+                mm(0, 1)
+            if s + 2 < NG:
+                x_transpose(s + 2, 0)
+                x_evac(s + 2, 0, False)
+            if 0 < s + 1 < NG:
+                mm(s + 1, 0)
+                mm(s + 1, 1)
+            if s == -1:
+                mm(0, 2)
+                mm(0, 3)
+            if s + 2 < NG:
+                x_transpose(s + 2, 1)
+            if 0 < s + 1 < NG:
+                mm(s + 1, 2)
+                mm(s + 1, 3)
             if s >= 0:
                 v2(a)
+                v1(b)
+            if s + 1 < NG:
+                h_transpose(a + GT)
+                mean(a + GT)
+                rstd(a + GT)
+            if s + 2 < NG:
+                x_evac(s + 2, 1, False)
+            if s >= 0:
                 v2(b)
-                v3(s)
+            if s + 1 < NG:
+                h_transpose(b + GT)
+                mean(b + GT)
+                rstd(b + GT)
+            if s >= 0:
+                v3(a)
+                v3(b)
 
         gm = const.tile([P, 4], F32, name="gm")
-        nc.vector.tensor_reduce(out=gm[:, 0:1], in_=am[:], axis=AX.X, op=ALU.max)
-        spread = psum.tile([P, P], F32, name="spread", tag="xt")
+        am_s = const.tile([P, NT], F32, name="am_s")
+        nc.vector.tensor_scalar(
+            out=am_s[:], in0=am[:], scalar1=1.0 / 448.0, scalar2=None, op0=ALU.mult, op1=ALU.max, accum_out=gm[:, 0:1]
+        )
+        spread = psum.tile([P, P], F32, name="spread", tag="xt", bufs=1)
         nc.tensor.transpose(spread[:], gm[:, 0:1].to_broadcast([P, P]), ident[:])
         nc.vector.tensor_reduce(out=gm[:, 1:2], in_=spread[:], axis=AX.X, op=ALU.max)
-        nc.vector.reciprocal(out=gm[:, 2:3], in_=gm[:, 1:2])
-        nc.vector.tensor_scalar(out=gm[:, 3:4], in0=gm[:, 2:3], scalar1=448.0, scalar2=None, op0=ALU.mult)
+        nc.vector.reciprocal(out=gm[:, 3:4], in_=gm[:, 1:2])
         factor = gm[:, 3:4]
 
         for s in range(NG):

@@ -1,3 +1,4 @@
+import math
 from contextlib import ExitStack
 
 import concourse.mybir as mybir
@@ -25,6 +26,7 @@ NTOK = GT * P
 KP = D // 512
 NJ = H // P
 HB = 512
+SQRT_H = math.sqrt(H)
 W_V_COLS = 256
 CAST_V_COLS = 1376
 
@@ -47,6 +49,11 @@ def tile_evidentialhead_pa_kernel(tc, x, W1, b1, g, beta, out_0, out_1):
         psum = ctx.enter_context(tc.psum_pool(name="psum", bufs=2))
         ctx.enter_context(tc.manual_schedule())
 
+        stage = const.tile([P, H], BF16, name="stage")
+        nc.vector.memset(stage[:], 0.0)
+        nc.scalar.dma_start(out=stage[0:1, :], in_=g.rearrange("(o c) -> o c", o=1))
+        nc.scalar.dma_start(out=stage[1:2, :], in_=beta.rearrange("(o c) -> o c", o=1))
+        nc.scalar.dma_start(out=stage[2 : 2 + NJ, 0:P], in_=b1.rearrange("(j p) -> j p", p=P))
         warm = const.tile([P, 2], F32, name="warm")
         nc.vector.memset(warm[:], 0.0)
         nc.scalar.activation(out=warm[:, 1:2], in_=warm[:, 0:1], func=ACT.Silu)
@@ -56,10 +63,8 @@ def tile_evidentialhead_pa_kernel(tc, x, W1, b1, g, beta, out_0, out_1):
         nc.vector.memset(mhalf[:], -0.5)
         ident = const.tile([P, P], F32, name="ident")
         make_identity(nc, ident[:])
-
-        b1_bf = const.tile([P, NJ], BF16, name="b1_bf")
-        with nc.allow_non_contiguous_dma(reason="one bias value to a partition"):
-            nc.scalar.dma_start(out=b1_bf[:], in_=b1.rearrange("(c p) -> p c", p=P))
+        ident_bf = const.tile([P, P], BF16, name="ident_bf")
+        make_identity(nc, ident_bf[:])
 
         xr = []
         wr = []
@@ -78,16 +83,12 @@ def tile_evidentialhead_pa_kernel(tc, x, W1, b1, g, beta, out_0, out_1):
                 in_=W1[512 * kp : 512 * (kp + 1), HB * hf : HB * (hf + 1)].rearrange("(p j) w -> p j w", j=4),
             )
             wr.append(t)
-        load_x(1)
-        g_bc = const.tile([P, H], BF16, name="g_bc")
-        nc.sync.dma_start(out=g_bc[:], in_=g.partition_broadcast(P))
-        beta_bc = const.tile([P, H], BF16, name="beta_bc")
-        nc.sync.dma_start(out=beta_bc[:], in_=beta.partition_broadcast(P))
-        for s in range(2, NG):
+        for s in range(1, NG):
             load_x(s)
 
         b1f = const.tile([P, NJ], F32, name="b1f")
-        nc.vector.tensor_copy(out=b1f[:], in_=b1_bf[:])
+        g_bc = const.tile([P, H], F32, name="g_bc")
+        beta_bc = const.tile([P, H], F32, name="beta_bc")
         am = const.tile([P, NT], F32, name="am")
 
         wc = {}
@@ -103,6 +104,31 @@ def tile_evidentialhead_pa_kernel(tc, x, W1, b1, g, beta, out_0, out_1):
         gs = {}
         tt = {}
         ob = {}
+        spread_ps = {}
+
+        def spread_rows():
+            ps = psum.tile([P, NJ], F32, name="b1_ps", tag="mu", bufs=1)
+            nc.tensor.matmul(out=ps[:], lhsT=stage[:, 0:P], rhs=ident_bf[:, 2 : 2 + NJ], start=True, stop=True)
+            nc.scalar.copy(out=b1f[:], in_=ps[:])
+            for row in range(2):
+                for half in range(2):
+                    ps = psum.tile([P, HB], F32, name="ht%d" % half, tag="ht%d" % half)
+                    nc.tensor.matmul(
+                        out=ps[:],
+                        lhsT=ident_bf[:, row : row + 1].to_broadcast([P, P]),
+                        rhs=stage[:, half * HB : (half + 1) * HB],
+                        start=True,
+                        stop=True,
+                    )
+                    spread_ps[(row, half)] = ps
+
+        def keep_rows():
+            for half in range(2):
+                cols = slice(half * HB, (half + 1) * HB)
+                nc.vector.tensor_scalar(out=g_bc[:, cols], in0=spread_ps[(0, half)][:], scalar1=SQRT_H, scalar2=None, op0=ALU.mult)
+            for half in range(2):
+                cols = slice(half * HB, (half + 1) * HB)
+                nc.vector.tensor_copy(out=beta_bc[:, cols], in_=spread_ps[(1, half)][:])
 
         def w_copy(c):
             t = wtmp.tile([P, HB, 4], BF16, name="wg", tag="wg", align_bytes=64)
@@ -117,7 +143,8 @@ def tile_evidentialhead_pa_kernel(tc, x, W1, b1, g, beta, out_0, out_1):
             wc[chunks[c]] = codes
             ws[chunks[c]] = scales
 
-        def x_transpose(s, tl):
+        def x_turn(i):
+            s, tl = i // GT, i % GT
             if tl == 0:
                 xg[s] = xprep.tile([P, KP, NTOK, 4], BF16, name="xg", tag="xg", align_bytes=64)
             ps = psum.tile([P, KP, 2, P], F32, name="xt", tag="xt", bufs=1)
@@ -125,16 +152,8 @@ def tile_evidentialhead_pa_kernel(tc, x, W1, b1, g, beta, out_0, out_1):
             for kp in range(KP):
                 for u in range(2):
                     nc.tensor.transpose(ps[:, kp, u, :], words[:, 256 * kp + u : 256 * (kp + 1) : 2], ident[:])
-            xt_ps[(s, tl)] = ps
-
-        def x_evac(s, tl, on_vector):
             dst = xg[s][:].rearrange("p k r e -> p (k r e)").bitcast(F32).rearrange("p (k r u) -> p k r u", k=KP, u=2)
-            dst = dst[:, :, tl * P : (tl + 1) * P, :]
-            src = xt_ps[(s, tl)][:].rearrange("p k u r -> p k r u")
-            if on_vector:
-                nc.vector.tensor_copy(out=dst, in_=src)
-            else:
-                nc.scalar.copy(out=dst, in_=src)
+            nc.scalar.copy(out=dst[:, :, tl * P : (tl + 1) * P, :], in_=ps[:].rearrange("p k u r -> p k r u"))
 
         def x_quant(s):
             xc[s] = xprep.tile([P, KP * NTOK], U32, name="xc", tag="xc", align_bytes=64)
@@ -165,49 +184,39 @@ def tile_evidentialhead_pa_kernel(tc, x, W1, b1, g, beta, out_0, out_1):
                 j = 2 * jp + jj
                 nc.scalar.activation(out=hs[s][:, j, :], in_=acc[:, jj, :], func=ACT.Silu, bias=b1f[:, j : j + 1], scale=1.0)
 
-        def h_transpose(i):
+        def h_turn(i):
             s, tl = i // GT, i % GT
+            toks = slice(tl * P, (tl + 1) * P)
             fold = psum.tile([P, P], F32, name="fold", tag="mu", bufs=1)
             for j in range(NJ):
                 nc.tensor.matmul(
-                    out=fold[:],
-                    lhsT=hs[s][:, j, tl * P : (tl + 1) * P],
-                    rhs=ident[:],
-                    is_transpose=True,
-                    start=(j == 0),
-                    stop=(j == NJ - 1),
+                    out=fold[:], lhsT=hs[s][:, j, toks], rhs=ident[:], is_transpose=True, start=(j == 0), stop=(j == NJ - 1)
                 )
-            fold_ps[i] = fold
             banks = []
             for half in range(2):
                 ps = psum.tile([P, HB], F32, name="ht%d" % half, tag="ht%d" % half)
                 for q in range(4):
-                    nc.tensor.transpose(ps[:, q * P : (q + 1) * P], hs[s][:, 4 * half + q, tl * P : (tl + 1) * P], ident[:])
+                    nc.tensor.transpose(ps[:, q * P : (q + 1) * P], hs[s][:, 4 * half + q, toks], ident[:])
                 banks.append(ps)
             ht_ps[i] = banks
-
-        def mean(i):
-            sp[i] = stat.tile([P, 4], F32, name="sp", tag="sp")
+            sp[i] = stat.tile([P, 2], F32, name="sp", tag="sp")
             gs[i] = stat.tile([P, 4], F32, name="gs", tag="gs")
             junk = stat.tile([P, HB], BF16, name="junk", tag="junk")
-            nc.scalar.activation(out=junk[:, 0:P], in_=fold_ps[i][:], func=ACT.Copy, scale=-1.0 / H, accum_out=gs[i][:, 0:1])
-
-        def rstd(i):
+            nc.scalar.activation(out=junk[:, 0:P], in_=fold[:], func=ACT.Copy, scale=-1.0 / H, accum_out=gs[i][:, 0:1])
             for half in range(2):
                 junk = stat.tile([P, HB], BF16, name="junk", tag="junk")
                 nc.scalar.activation(
                     out=junk[:],
-                    in_=ht_ps[i][half][:],
+                    in_=banks[half][:],
                     func=ACT.Square,
                     bias=gs[i][:, 0:1],
                     scale=1.0,
-                    accum_out=sp[i][:, 2 + half : 3 + half],
+                    accum_out=sp[i][:, half : half + 1],
                 )
             nc.gpsimd.tensor_scalar(
-                out=gs[i][:, 1:2], in0=sp[i][:, 2:3], scalar1=sp[i][:, 3:4], scalar2=1.0 / H, op0=ALU.add, op1=ALU.mult
+                out=gs[i][:, 1:2], in0=sp[i][:, 0:1], scalar1=sp[i][:, 1:2], scalar2=H * EPS_LN, op0=ALU.add, op1=ALU.add
             )
-            nc.gpsimd.tensor_scalar(out=gs[i][:, 2:3], in0=gs[i][:, 1:2], scalar1=1.0, scalar2=EPS_LN, op0=ALU.mult, op1=ALU.add)
-            nc.gpsimd.tensor_tensor(out=gs[i][:, 3:4], in0=gs[i][:, 2:3], in1=mhalf[:], op=ALU.pow)
+            nc.gpsimd.tensor_tensor(out=gs[i][:, 2:3], in0=gs[i][:, 1:2], in1=mhalf[:], op=ALU.pow)
 
         def v1(i):
             tt[i] = work.tile([P, H], F32, name="t", tag="t")
@@ -222,7 +231,7 @@ def tile_evidentialhead_pa_kernel(tc, x, W1, b1, g, beta, out_0, out_1):
             if tl == 0:
                 ob[s] = opool.tile([P, GT, H], F32, name="o", tag="o")
             nc.vector.scalar_tensor_tensor(
-                out=ob[s][:, tl, :], in0=tt[i][:], scalar=gs[i][:, 3:4], in1=beta_bc[:], op0=ALU.mult, op1=ALU.add
+                out=ob[s][:, tl, :], in0=tt[i][:], scalar=gs[i][:, 2:3], in1=beta_bc[:], op0=ALU.mult, op1=ALU.add
             )
             if tl == GT - 1:
                 nc.sync.dma_start(out=o0_v[:, GT * s : GT * (s + 1), :], in_=ob[s][:])
@@ -233,12 +242,19 @@ def tile_evidentialhead_pa_kernel(tc, x, W1, b1, g, beta, out_0, out_1):
                 out=am[:, i : i + 1], in_=ob[s][:, tl, :], axis=AX.X, op=ALU.max, apply_absolute_value=True
             )
 
-        x_transpose(0, 0)
-        x_evac(0, 0, False)
+        def v_step(i):
+            if i < NT:
+                v1(i)
+            if 0 <= i - 1 < NT:
+                v2(i - 1)
+            if 0 <= i - 2 < NT:
+                v3(i - 2)
+
+        x_turn(0)
         t0 = w_copy(0)
-        x_transpose(0, 1)
-        x_evac(0, 1, False)
+        x_turn(1)
         t1 = w_copy(1)
+        spread_rows()
         w_quant(0, t0)
         x_quant(0)
         t2 = w_copy(2)
@@ -246,47 +262,35 @@ def tile_evidentialhead_pa_kernel(tc, x, W1, b1, g, beta, out_0, out_1):
         t3 = w_copy(3)
         w_quant(2, t2)
         w_quant(3, t3)
-        for s in range(-1, NG):
+        mm(0, 0)
+        mm(0, 1)
+        x_turn(2)
+        mm(0, 2)
+        mm(0, 3)
+        x_turn(3)
+        keep_rows()
+        x_quant(1)
+        h_turn(0)
+        h_turn(1)
+        for s in range(NG + 1):
             a, b = GT * s, GT * s + 1
-            if s >= 0:
-                v1(a)
-            if 0 < s + 1 < NG:
-                x_quant(s + 1)
-            if s == -1:
-                mm(0, 0)
-                mm(0, 1)
-            if s + 2 < NG:
-                x_transpose(s + 2, 0)
-                x_evac(s + 2, 0, False)
-            if 0 < s + 1 < NG:
+            v_step(a)
+            if a + 4 < NT:
+                x_turn(a + 4)
+            if s + 1 < NG:
                 mm(s + 1, 0)
                 mm(s + 1, 1)
-            if s == -1:
-                mm(0, 2)
-                mm(0, 3)
-            if s + 2 < NG:
-                x_transpose(s + 2, 1)
-            if 0 < s + 1 < NG:
+            if b + 4 < NT:
+                x_turn(b + 4)
+            if s + 1 < NG:
                 mm(s + 1, 2)
                 mm(s + 1, 3)
-            if s >= 0:
-                v2(a)
-                v1(b)
-            if s + 1 < NG:
-                h_transpose(a + GT)
-                mean(a + GT)
-                rstd(a + GT)
             if s + 2 < NG:
-                x_evac(s + 2, 1, False)
-            if s >= 0:
-                v2(b)
-            if s + 1 < NG:
-                h_transpose(b + GT)
-                mean(b + GT)
-                rstd(b + GT)
-            if s >= 0:
-                v3(a)
-                v3(b)
+                x_quant(s + 2)
+            v_step(b)
+            if a + 2 < NT:
+                h_turn(a + 2)
+                h_turn(b + 2)
 
         gm = const.tile([P, 4], F32, name="gm")
         am_s = const.tile([P, NT], F32, name="am_s")

@@ -28,6 +28,7 @@ NJ = H // P
 HB = 512
 SQRT_H = math.sqrt(H)
 W_V_COLS = 256
+V_STAT_TILES = 2
 CAST_V_COLS = 1376
 
 
@@ -187,11 +188,12 @@ def tile_evidentialhead_pa_kernel(tc, x, W1, b1, g, beta, out_0, out_1):
         def h_turn(i):
             s, tl = i // GT, i % GT
             toks = slice(tl * P, (tl + 1) * P)
-            fold = psum.tile([P, P], F32, name="fold", tag="mu", bufs=1)
-            for j in range(NJ):
-                nc.tensor.matmul(
-                    out=fold[:], lhsT=hs[s][:, j, toks], rhs=ident[:], is_transpose=True, start=(j == 0), stop=(j == NJ - 1)
-                )
+            if i >= V_STAT_TILES:
+                fold = psum.tile([P, P], F32, name="fold", tag="mu", bufs=1)
+                for j in range(NJ):
+                    nc.tensor.matmul(
+                        out=fold[:], lhsT=hs[s][:, j, toks], rhs=ident[:], is_transpose=True, start=(j == 0), stop=(j == NJ - 1)
+                    )
             banks = []
             for half in range(2):
                 ps = psum.tile([P, HB], F32, name="ht%d" % half, tag="ht%d" % half)
@@ -199,8 +201,20 @@ def tile_evidentialhead_pa_kernel(tc, x, W1, b1, g, beta, out_0, out_1):
                     nc.tensor.transpose(ps[:, q * P : (q + 1) * P], hs[s][:, 4 * half + q, toks], ident[:])
                 banks.append(ps)
             ht_ps[i] = banks
-            sp[i] = stat.tile([P, 2], F32, name="sp", tag="sp")
             gs[i] = stat.tile([P, 4], F32, name="gs", tag="gs")
+            if i < V_STAT_TILES:
+                bn = stat.tile([P, 2, 6], F32, name="bn", tag="bn")
+                for half in range(2):
+                    nc.vector.bn_stats(out=bn[:, half, :], in_=banks[half][:])
+                mv = stat.tile([P, 2], F32, name="mv", tag="mv")
+                nc.vector.bn_aggr(out=mv[:], in_=bn[:].rearrange("p a b -> p (a b)"))
+                nc.gpsimd.tensor_scalar(out=gs[i][:, 0:1], in0=mv[:, 0:1], scalar1=-1.0, scalar2=0.0, op0=ALU.mult, op1=ALU.add)
+                nc.gpsimd.tensor_scalar(
+                    out=gs[i][:, 1:2], in0=mv[:, 1:2], scalar1=float(H), scalar2=H * EPS_LN, op0=ALU.mult, op1=ALU.add
+                )
+                nc.gpsimd.tensor_tensor(out=gs[i][:, 2:3], in0=gs[i][:, 1:2], in1=mhalf[:], op=ALU.pow)
+                return
+            sp[i] = stat.tile([P, 2], F32, name="sp", tag="sp")
             junk = stat.tile([P, HB], BF16, name="junk", tag="junk")
             nc.scalar.activation(out=junk[:, 0:P], in_=fold[:], func=ACT.Copy, scale=-1.0 / H, accum_out=gs[i][:, 0:1])
             for half in range(2):
@@ -285,11 +299,12 @@ def tile_evidentialhead_pa_kernel(tc, x, W1, b1, g, beta, out_0, out_1):
             if s + 1 < NG:
                 mm(s + 1, 2)
                 mm(s + 1, 3)
-            if s + 2 < NG:
-                x_quant(s + 2)
             v_step(b)
             if a + 2 < NT:
                 h_turn(a + 2)
+            if s + 2 < NG:
+                x_quant(s + 2)
+            if a + 2 < NT:
                 h_turn(b + 2)
 
         gm = const.tile([P, 4], F32, name="gm")

@@ -257,7 +257,7 @@ def tile_evidentialhead_pa_kernel(tc, x, W1, b1, g, beta, out_0, out_1):
             )
 
         def v_step(i):
-            if i < NT:
+            if 0 <= i < NT:
                 v1(i)
             if 0 <= i - 1 < NT:
                 v2(i - 1)
@@ -284,28 +284,20 @@ def tile_evidentialhead_pa_kernel(tc, x, W1, b1, g, beta, out_0, out_1):
         x_turn(3)
         keep_rows()
         x_quant(1)
-        h_turn(0)
-        h_turn(1)
-        for s in range(NG + 1):
-            a, b = GT * s, GT * s + 1
-            v_step(a)
-            if a + 4 < NT:
-                x_turn(a + 4)
+        for t in range(NT + 4):
+            s, tl = t // GT, t % GT
+            v_step(t - 2)
+            if tl == 0 and 2 <= s + 1 < NG:
+                x_quant(s + 1)
+            if t < V_STAT_TILES:
+                h_turn(t)
+            if t + 4 < NT:
+                x_turn(t + 4)
+            if V_STAT_TILES <= t < NT:
+                h_turn(t)
             if s + 1 < NG:
-                mm(s + 1, 0)
-                mm(s + 1, 1)
-            if b + 4 < NT:
-                x_turn(b + 4)
-            if s + 1 < NG:
-                mm(s + 1, 2)
-                mm(s + 1, 3)
-            v_step(b)
-            if a + 2 < NT:
-                h_turn(a + 2)
-            if s + 2 < NG:
-                x_quant(s + 2)
-            if a + 2 < NT:
-                h_turn(b + 2)
+                mm(s + 1, 2 * tl)
+                mm(s + 1, 2 * tl + 1)
 
         gm = const.tile([P, 4], F32, name="gm")
         am_s = const.tile([P, NT], F32, name="am_s")

@@ -27,7 +27,7 @@ KP = D // 512
 NJ = H // P
 HB = 512
 SQRT_H = math.sqrt(H)
-W_V_COLS = 256
+W_V_COLS = 288
 V_STAT_TILES = 2
 CAST_V_COLS = 1376
 
@@ -76,8 +76,12 @@ def tile_evidentialhead_pa_kernel(tc, x, W1, b1, g, beta, out_0, out_1):
             xr.append(t)
 
         chunks = [(0, 0), (1, 0), (0, 1), (1, 1)]
-        load_x(0)
-        for kp, hf in chunks:
+        x0 = xraw.tile([P, GT, D], BF16, name="xr", tag="xr")
+        xr.append(x0)
+        nc.sync.dma_start(out=x0[:, 0:1, :], in_=x_v[:, 0:1, :])
+        for n, (kp, hf) in enumerate(chunks):
+            if n == 1:
+                nc.sync.dma_start(out=x0[:, 1:2, :], in_=x_v[:, 1:2, :])
             t = wtmp.tile([P, 4, HB], BF16, name="wr", tag="wr")
             nc.sync.dma_start(
                 out=t[:],
@@ -103,6 +107,7 @@ def tile_evidentialhead_pa_kernel(tc, x, W1, b1, g, beta, out_0, out_1):
         fold_ps = {}
         sp = {}
         gs = {}
+        mean = {}
         tt = {}
         ob = {}
         spread_ps = {}
@@ -208,7 +213,7 @@ def tile_evidentialhead_pa_kernel(tc, x, W1, b1, g, beta, out_0, out_1):
                     nc.vector.bn_stats(out=bn[:, half, :], in_=banks[half][:])
                 mv = stat.tile([P, 2], F32, name="mv", tag="mv")
                 nc.vector.bn_aggr(out=mv[:], in_=bn[:].rearrange("p a b -> p (a b)"))
-                nc.gpsimd.tensor_scalar(out=gs[i][:, 0:1], in0=mv[:, 0:1], scalar1=-1.0, scalar2=0.0, op0=ALU.mult, op1=ALU.add)
+                mean[i] = mv
                 nc.gpsimd.tensor_scalar(
                     out=gs[i][:, 1:2], in0=mv[:, 1:2], scalar1=float(H), scalar2=H * EPS_LN, op0=ALU.mult, op1=ALU.add
                 )
@@ -236,9 +241,14 @@ def tile_evidentialhead_pa_kernel(tc, x, W1, b1, g, beta, out_0, out_1):
             tt[i] = work.tile([P, H], F32, name="t", tag="t")
             for half in range(2):
                 cols = slice(half * HB, (half + 1) * HB)
-                nc.vector.scalar_tensor_tensor(
-                    out=tt[i][:, cols], in0=ht_ps[i][half][:], scalar=gs[i][:, 0:1], in1=g_bc[:, cols], op0=ALU.add, op1=ALU.mult
-                )
+                if i in mean:
+                    nc.vector.scalar_tensor_tensor(
+                        out=tt[i][:, cols], in0=ht_ps[i][half][:], scalar=mean[i][:, 0:1], in1=g_bc[:, cols], op0=ALU.subtract, op1=ALU.mult
+                    )
+                else:
+                    nc.vector.scalar_tensor_tensor(
+                        out=tt[i][:, cols], in0=ht_ps[i][half][:], scalar=gs[i][:, 0:1], in1=g_bc[:, cols], op0=ALU.add, op1=ALU.mult
+                    )
 
         def v2(i):
             s, tl = i // GT, i % GT
@@ -289,8 +299,9 @@ def tile_evidentialhead_pa_kernel(tc, x, W1, b1, g, beta, out_0, out_1):
             v_step(t - 2)
             if tl == 0 and 2 <= s + 1 < NG:
                 x_quant(s + 1)
-            if t < V_STAT_TILES:
-                h_turn(t)
+            if t == 0:
+                for i in range(V_STAT_TILES):
+                    h_turn(i)
             if t + 4 < NT:
                 x_turn(t + 4)
             if V_STAT_TILES <= t < NT:

@@ -29,6 +29,7 @@ HB = 512
 SQRT_H = math.sqrt(H)
 W_V_COLS = 288
 V_STAT_TILES = 2
+P_TILES = (14,)
 CAST_V_COLS = 1376
 
 
@@ -55,6 +56,8 @@ def tile_evidentialhead_pa_kernel(tc, x, W1, b1, g, beta, out_0, out_1):
         nc.scalar.dma_start(out=stage[0:1, :], in_=g.rearrange("(o c) -> o c", o=1))
         nc.scalar.dma_start(out=stage[1:2, :], in_=beta.rearrange("(o c) -> o c", o=1))
         nc.scalar.dma_start(out=stage[2 : 2 + NJ, 0:P], in_=b1.rearrange("(j p) -> j p", p=P))
+        nc.scalar.dma_start(out=stage[2 + NJ : 2 + 2 * NJ, 0:P], in_=g.rearrange("(j p) -> j p", p=P))
+        nc.scalar.dma_start(out=stage[2 + 2 * NJ : 2 + 3 * NJ, 0:P], in_=beta.rearrange("(j p) -> j p", p=P))
         warm = const.tile([P, 2], F32, name="warm")
         nc.vector.memset(warm[:], 0.0)
         nc.scalar.activation(out=warm[:, 1:2], in_=warm[:, 0:1], func=ACT.Silu)
@@ -91,7 +94,8 @@ def tile_evidentialhead_pa_kernel(tc, x, W1, b1, g, beta, out_0, out_1):
         for s in range(1, NG):
             load_x(s)
 
-        b1f = const.tile([P, NJ], F32, name="b1f")
+        b1f = const.tile([P, 3 * NJ], F32, name="b1f")
+        g_col = const.tile([P, NJ], F32, name="g_col")
         g_bc = const.tile([P, H], F32, name="g_bc")
         beta_bc = const.tile([P, H], F32, name="beta_bc")
         am = const.tile([P, NT], F32, name="am")
@@ -113,9 +117,10 @@ def tile_evidentialhead_pa_kernel(tc, x, W1, b1, g, beta, out_0, out_1):
         spread_ps = {}
 
         def spread_rows():
-            ps = psum.tile([P, NJ], F32, name="b1_ps", tag="mu", bufs=1)
-            nc.tensor.matmul(out=ps[:], lhsT=stage[:, 0:P], rhs=ident_bf[:, 2 : 2 + NJ], start=True, stop=True)
+            ps = psum.tile([P, 3 * NJ], F32, name="b1_ps", tag="mu", bufs=1)
+            nc.tensor.matmul(out=ps[:], lhsT=stage[:, 0:P], rhs=ident_bf[:, 2 : 2 + 3 * NJ], start=True, stop=True)
             nc.scalar.copy(out=b1f[:], in_=ps[:])
+            nc.scalar.activation(out=g_col[:], in_=ps[:, NJ : 2 * NJ], func=ACT.Copy, scale=SQRT_H)
             for row in range(2):
                 for half in range(2):
                     ps = psum.tile([P, HB], F32, name="ht%d" % half, tag="ht%d" % half)
@@ -237,6 +242,50 @@ def tile_evidentialhead_pa_kernel(tc, x, W1, b1, g, beta, out_0, out_1):
             )
             nc.gpsimd.tensor_tensor(out=gs[i][:, 2:3], in0=gs[i][:, 1:2], in1=mhalf[:], op=ALU.pow)
 
+        zt = {}
+        zT = {}
+        oT = {}
+
+        def p_norm(i):
+            nc.scalar.activation(out=gs[i][:, 3:4], in_=gs[i][:, 0:1], func=ACT.Copy, scale=gs[i][:, 2:3])
+            zt[i] = work.tile([P, H], F32, name="zt", tag="zt", bufs=1)
+            for half in range(2):
+                cols = slice(half * HB, (half + 1) * HB)
+                nc.scalar.activation(
+                    out=zt[i][:, cols], in_=ht_ps[i][half][:], func=ACT.Identity, scale=gs[i][:, 2:3], bias=gs[i][:, 3:4]
+                )
+
+        def p_back(i):
+            zT[i] = []
+            for half in range(2):
+                ps = psum.tile([P, 4, P], F32, name="zT", tag="acc")
+                for q in range(4):
+                    j = 4 * half + q
+                    nc.tensor.transpose(ps[:, q, :], zt[i][:, j * P : (j + 1) * P], ident[:])
+                zT[i].append(ps)
+
+        def p_affine(i):
+            oT[i] = work.tile([P, H], F32, name="oT", tag="oT", bufs=1)
+            for j in range(NJ):
+                nc.scalar.activation(
+                    out=oT[i][:, j * P : (j + 1) * P],
+                    in_=zT[i][j // 4][:, j % 4, :],
+                    func=ACT.Identity,
+                    scale=g_col[:, j : j + 1],
+                    bias=b1f[:, 2 * NJ + j : 2 * NJ + j + 1],
+                )
+
+        def p_out(i):
+            s, tl = i // GT, i % GT
+            if tl == 0:
+                ob[s] = opool.tile([P, GT, H], F32, name="o", tag="o")
+            for half in range(2):
+                ps = psum.tile([P, HB], F32, name="ht%d" % half, tag="ht%d" % half)
+                for q in range(4):
+                    j = 4 * half + q
+                    nc.tensor.transpose(ps[:, q * P : (q + 1) * P], oT[i][:, j * P : (j + 1) * P], ident[:])
+                nc.scalar.copy(out=ob[s][:, tl, half * HB : (half + 1) * HB], in_=ps[:])
+
         def v1(i):
             tt[i] = work.tile([P, H], F32, name="t", tag="t")
             for half in range(2):
@@ -267,11 +316,11 @@ def tile_evidentialhead_pa_kernel(tc, x, W1, b1, g, beta, out_0, out_1):
             )
 
         def v_step(i):
-            if 0 <= i < NT:
+            if 0 <= i < NT and i not in P_TILES:
                 v1(i)
-            if 0 <= i - 1 < NT:
+            if 0 <= i - 1 < NT and i - 1 not in P_TILES:
                 v2(i - 1)
-            if 0 <= i - 2 < NT:
+            if 0 <= i - 2 < NT and i - 2 not in P_TILES:
                 v3(i - 2)
 
         x_turn(0)
@@ -306,9 +355,17 @@ def tile_evidentialhead_pa_kernel(tc, x, W1, b1, g, beta, out_0, out_1):
                 x_turn(t + 4)
             if V_STAT_TILES <= t < NT:
                 h_turn(t)
+            if t - 1 in P_TILES:
+                p_norm(t - 1)
+                p_back(t - 1)
+                p_affine(t - 1)
+                p_out(t - 1)
             if s + 1 < NG:
                 mm(s + 1, 2 * tl)
                 mm(s + 1, 2 * tl + 1)
+
+        for i in P_TILES:
+            v3(i)
 
         gm = const.tile([P, 4], F32, name="gm")
         am_s = const.tile([P, NT], F32, name="am_s")

@@ -154,7 +154,7 @@ def tile_evidentialhead_pa_kernel(tc, x, W1, b1, g, beta, out_0, out_1):
             wc[chunks[c]] = codes
             ws[chunks[c]] = scales
 
-        def x_turn(i):
+        def x_T(i):
             s, tl = i // GT, i % GT
             if tl == 0:
                 xg[s] = xprep.tile([P, KP, NTOK, 4], BF16, name="xg", tag="xg", align_bytes=64)
@@ -163,8 +163,16 @@ def tile_evidentialhead_pa_kernel(tc, x, W1, b1, g, beta, out_0, out_1):
             for kp in range(KP):
                 for u in range(2):
                     nc.tensor.transpose(ps[:, kp, u, :], words[:, 256 * kp + u : 256 * (kp + 1) : 2], ident[:])
+            xt_ps[i] = ps
+
+        def x_copy(i):
+            s, tl = i // GT, i % GT
             dst = xg[s][:].rearrange("p k r e -> p (k r e)").bitcast(F32).rearrange("p (k r u) -> p k r u", k=KP, u=2)
-            nc.scalar.copy(out=dst[:, :, tl * P : (tl + 1) * P, :], in_=ps[:].rearrange("p k u r -> p k r u"))
+            nc.scalar.copy(out=dst[:, :, tl * P : (tl + 1) * P, :], in_=xt_ps[i][:].rearrange("p k u r -> p k r u"))
+
+        def x_turn(i):
+            x_T(i)
+            x_copy(i)
 
         def x_quant(s):
             xc[s] = xprep.tile([P, KP * NTOK], U32, name="xc", tag="xc", align_bytes=64)
@@ -195,15 +203,24 @@ def tile_evidentialhead_pa_kernel(tc, x, W1, b1, g, beta, out_0, out_1):
                 j = 2 * jp + jj
                 nc.scalar.activation(out=hs[s][:, j, :], in_=acc[:, jj, :], func=ACT.Silu, bias=b1f[:, j : j + 1], scale=1.0)
 
-        def h_turn(i):
+        def fold_T(i):
             s, tl = i // GT, i % GT
             toks = slice(tl * P, (tl + 1) * P)
-            if i >= V_STAT_TILES:
-                fold = psum.tile([P, P], F32, name="fold", tag="mu", bufs=1)
-                for j in range(NJ):
-                    nc.tensor.matmul(
-                        out=fold[:], lhsT=hs[s][:, j, toks], rhs=ident[:], is_transpose=True, start=(j == 0), stop=(j == NJ - 1)
-                    )
+            fold = psum.tile([P, P], F32, name="fold", tag="mu", bufs=1)
+            for j in range(NJ):
+                nc.tensor.matmul(
+                    out=fold[:], lhsT=hs[s][:, j, toks], rhs=ident[:], is_transpose=True, start=(j == 0), stop=(j == NJ - 1)
+                )
+            fold_ps[i] = fold
+
+        def fold_copy(i):
+            gs[i] = stat.tile([P, 4], F32, name="gs", tag="gs")
+            junk = stat.tile([P, HB], BF16, name="junk", tag="junk")
+            nc.scalar.activation(out=junk[:, 0:P], in_=fold_ps[i][:], func=ACT.Copy, scale=-1.0 / H, accum_out=gs[i][:, 0:1])
+
+        def h_T(i):
+            s, tl = i // GT, i % GT
+            toks = slice(tl * P, (tl + 1) * P)
             banks = []
             for half in range(2):
                 ps = psum.tile([P, HB], F32, name="ht%d" % half, tag="ht%d" % half)
@@ -211,22 +228,24 @@ def tile_evidentialhead_pa_kernel(tc, x, W1, b1, g, beta, out_0, out_1):
                     nc.tensor.transpose(ps[:, q * P : (q + 1) * P], hs[s][:, 4 * half + q, toks], ident[:])
                 banks.append(ps)
             ht_ps[i] = banks
+
+        def v_stats(i):
+            banks = ht_ps[i]
             gs[i] = stat.tile([P, 4], F32, name="gs", tag="gs")
-            if i < V_STAT_TILES:
-                bn = stat.tile([P, 2, 6], F32, name="bn", tag="bn")
-                for half in range(2):
-                    nc.vector.bn_stats(out=bn[:, half, :], in_=banks[half][:])
-                mv = stat.tile([P, 2], F32, name="mv", tag="mv")
-                nc.vector.bn_aggr(out=mv[:], in_=bn[:].rearrange("p a b -> p (a b)"))
-                mean[i] = mv
-                nc.gpsimd.tensor_scalar(
-                    out=gs[i][:, 1:2], in0=mv[:, 1:2], scalar1=float(H), scalar2=H * EPS_LN, op0=ALU.mult, op1=ALU.add
-                )
-                nc.gpsimd.tensor_tensor(out=gs[i][:, 2:3], in0=gs[i][:, 1:2], in1=mhalf[:], op=ALU.pow)
-                return
+            bn = stat.tile([P, 2, 6], F32, name="bn", tag="bn")
+            for half in range(2):
+                nc.vector.bn_stats(out=bn[:, half, :], in_=banks[half][:])
+            mv = stat.tile([P, 2], F32, name="mv", tag="mv")
+            nc.vector.bn_aggr(out=mv[:], in_=bn[:].rearrange("p a b -> p (a b)"))
+            mean[i] = mv
+            nc.gpsimd.tensor_scalar(
+                out=gs[i][:, 1:2], in0=mv[:, 1:2], scalar1=float(H), scalar2=H * EPS_LN, op0=ALU.mult, op1=ALU.add
+            )
+            nc.gpsimd.tensor_tensor(out=gs[i][:, 2:3], in0=gs[i][:, 1:2], in1=mhalf[:], op=ALU.pow)
+
+        def squares(i):
+            banks = ht_ps[i]
             sp[i] = stat.tile([P, 2], F32, name="sp", tag="sp")
-            junk = stat.tile([P, HB], BF16, name="junk", tag="junk")
-            nc.scalar.activation(out=junk[:, 0:P], in_=fold[:], func=ACT.Copy, scale=-1.0 / H, accum_out=gs[i][:, 0:1])
             for half in range(2):
                 junk = stat.tile([P, HB], BF16, name="junk", tag="junk")
                 nc.scalar.activation(
@@ -350,11 +369,20 @@ def tile_evidentialhead_pa_kernel(tc, x, W1, b1, g, beta, out_0, out_1):
                 x_quant(s + 1)
             if t == 0:
                 for i in range(V_STAT_TILES):
-                    h_turn(i)
-            if t + 4 < NT:
-                x_turn(t + 4)
-            if V_STAT_TILES <= t < NT:
-                h_turn(t)
+                    h_T(i)
+                    v_stats(i)
+            has_x = t + 4 < NT
+            has_h = V_STAT_TILES <= t < NT
+            if has_x:
+                x_T(t + 4)
+            if has_h:
+                fold_T(t)
+                fold_copy(t)
+            if has_x:
+                x_copy(t + 4)
+            if has_h:
+                h_T(t)
+                squares(t)
             if t - 1 in P_TILES:
                 p_norm(t - 1)
                 p_back(t - 1)

import math
from contextlib import ExitStack

import concourse.mybir as mybir
from concourse.masks import make_identity

B, D, H = 2048, 1024, 1024
EPS_LN = 1e-5
FLOPS = 2 * B * D * H

F32 = mybir.dt.float32
BF16 = mybir.dt.bfloat16
U32 = mybir.dt.uint32
U8 = mybir.dt.uint8
FP8X4 = mybir.dt.float8_e4m3fn_x4
FP8 = mybir.dt.float8_e4m3fn
ALU = mybir.AluOpType
ACT = mybir.ActivationFunctionType
AX = mybir.AxisListType

P = 128
NT = B // P
GT = 2
NG = NT // GT
NTOK = GT * P
KP = D // 512
NJ = H // P
HB = 512
SQRT_H = math.sqrt(H)
W_V_COLS = 288
V_STAT_TILES = 2
P_TILES = (14,)
CAST_V_COLS = 1376


def tile_evidentialhead_pa_kernel(tc, x, W1, b1, g, beta, out_0, out_1):
    nc = tc.nc
    x_v = x.rearrange("(p i) k -> p i k", i=NT)
    o0_v = out_0.rearrange("(p i) c -> p i c", i=NT)
    o1_v = out_1.rearrange("(p i) c -> p (i c)", i=NT)

    with ExitStack() as ctx:
        const = ctx.enter_context(tc.tile_pool(name="const", bufs=1))
        xraw = ctx.enter_context(tc.tile_pool(name="xraw", bufs=NG))
        wtmp = ctx.enter_context(tc.tile_pool(name="wtmp", bufs=4))
        xprep = ctx.enter_context(tc.tile_pool(name="xprep", bufs=2))
        hpool = ctx.enter_context(tc.tile_pool(name="hpool", bufs=2))
        work = ctx.enter_context(tc.tile_pool(name="work", bufs=2))
        stat = ctx.enter_context(tc.tile_pool(name="stat", bufs=4))
        opool = ctx.enter_context(tc.tile_pool(name="opool", bufs=NG))
        psum = ctx.enter_context(tc.psum_pool(name="psum", bufs=2))
        ctx.enter_context(tc.manual_schedule())

        stage = const.tile([P, H], BF16, name="stage")
        nc.vector.memset(stage[:], 0.0)
        nc.scalar.dma_start(out=stage[0:1, :], in_=g.rearrange("(o c) -> o c", o=1))
        nc.scalar.dma_start(out=stage[1:2, :], in_=beta.rearrange("(o c) -> o c", o=1))
        nc.scalar.dma_start(out=stage[2 : 2 + NJ, 0:P], in_=b1.rearrange("(j p) -> j p", p=P))
        nc.scalar.dma_start(out=stage[2 + NJ : 2 + 2 * NJ, 0:P], in_=g.rearrange("(j p) -> j p", p=P))
        nc.scalar.dma_start(out=stage[2 + 2 * NJ : 2 + 3 * NJ, 0:P], in_=beta.rearrange("(j p) -> j p", p=P))
        warm = const.tile([P, 2], F32, name="warm")
        nc.vector.memset(warm[:], 0.0)
        nc.scalar.activation(out=warm[:, 1:2], in_=warm[:, 0:1], func=ACT.Silu)
        zero = const.tile([P, 1], F32, name="zero")
        nc.vector.memset(zero[:], 0.0)
        mhalf = const.tile([P, 1], F32, name="mhalf")
        nc.vector.memset(mhalf[:], -0.5)
        ident = const.tile([P, P], F32, name="ident")
        make_identity(nc, ident[:])
        ident_bf = const.tile([P, P], BF16, name="ident_bf")
        make_identity(nc, ident_bf[:])

        xr = []
        wr = []

        def load_x(s):
            t = xraw.tile([P, GT, D], BF16, name="xr", tag="xr")
            nc.sync.dma_start(out=t[:], in_=x_v[:, GT * s : GT * (s + 1), :])
            xr.append(t)

        chunks = [(0, 0), (1, 0), (0, 1), (1, 1)]
        x0 = xraw.tile([P, GT, D], BF16, name="xr", tag="xr")
        xr.append(x0)
        nc.sync.dma_start(out=x0[:, 0:1, :], in_=x_v[:, 0:1, :])
        for n, (kp, hf) in enumerate(chunks):
            if n == 1:
                nc.sync.dma_start(out=x0[:, 1:2, :], in_=x_v[:, 1:2, :])
            t = wtmp.tile([P, 4, HB], BF16, name="wr", tag="wr")
            nc.sync.dma_start(
                out=t[:],
                in_=W1[512 * kp : 512 * (kp + 1), HB * hf : HB * (hf + 1)].rearrange("(p j) w -> p j w", j=4),
            )
            wr.append(t)
        for s in range(1, NG):
            load_x(s)

        b1f = const.tile([P, 3 * NJ], F32, name="b1f")
        g_col = const.tile([P, NJ], F32, name="g_col")
        g_bc = const.tile([P, H], F32, name="g_bc")
        beta_bc = const.tile([P, H], F32, name="beta_bc")
        am = const.tile([P, NT], F32, name="am")

        wc = {}
        ws = {}
        xt_ps = {}
        xg = {}
        xc = {}
        xs = {}
        hs = {}
        ht_ps = {}
        fold_ps = {}
        sp = {}
        gs = {}
        mean = {}
        tt = {}
        ob = {}
        spread_ps = {}

        def spread_rows():
            ps = psum.tile([P, 3 * NJ], F32, name="b1_ps", tag="mu", bufs=1)
            nc.tensor.matmul(out=ps[:], lhsT=stage[:, 0:P], rhs=ident_bf[:, 2 : 2 + 3 * NJ], start=True, stop=True)
            nc.scalar.copy(out=b1f[:], in_=ps[:])
            nc.scalar.activation(out=g_col[:], in_=ps[:, NJ : 2 * NJ], func=ACT.Copy, scale=SQRT_H)
            for row in range(2):
                for half in range(2):
                    ps = psum.tile([P, HB], F32, name="ht%d" % half, tag="ht%d" % half)
                    nc.tensor.matmul(
                        out=ps[:],
                        lhsT=ident_bf[:, row : row + 1].to_broadcast([P, P]),
                        rhs=stage[:, half * HB : (half + 1) * HB],
                        start=True,
                        stop=True,
                    )
                    spread_ps[(row, half)] = ps

        def keep_rows():
            for half in range(2):
                cols = slice(half * HB, (half + 1) * HB)
                nc.vector.tensor_scalar(out=g_bc[:, cols], in0=spread_ps[(0, half)][:], scalar1=SQRT_H, scalar2=None, op0=ALU.mult)
            for half in range(2):
                cols = slice(half * HB, (half + 1) * HB)
                nc.vector.tensor_copy(out=beta_bc[:, cols], in_=spread_ps[(1, half)][:])

        def w_copy(c):
            t = wtmp.tile([P, HB, 4], BF16, name="wg", tag="wg", align_bytes=64)
            nc.vector.tensor_copy(out=t[:, 0:W_V_COLS, :], in_=wr[c][:, :, 0:W_V_COLS].rearrange("p j w -> p w j"))
            nc.scalar.copy(out=t[:, W_V_COLS:HB, :], in_=wr[c][:, :, W_V_COLS:HB].rearrange("p j w -> p w j"))
            return t

        def w_quant(c, t):
            codes = const.tile([P, HB], U32, name="wc%d" % c, align_bytes=64)
            scales = const.tile([P, HB], U8, name="ws%d" % c, align_bytes=64)
            nc.vector.quantize_mx(out=codes[:].bitcast(FP8X4), scales=scales[:], in_=t[:].rearrange("p w j -> p (w j)"))
            wc[chunks[c]] = codes
            ws[chunks[c]] = scales

        def x_T(i):
            s, tl = i // GT, i % GT
            if tl == 0:
                xg[s] = xprep.tile([P, KP, NTOK, 4], BF16, name="xg", tag="xg", align_bytes=64)
            ps = psum.tile([P, KP, 2, P], F32, name="xt", tag="xt", bufs=1)
            words = xr[s][:, tl, :].bitcast(F32)
            for kp in range(KP):
                for u in range(2):
                    nc.tensor.transpose(ps[:, kp, u, :], words[:, 256 * kp + u : 256 * (kp + 1) : 2], ident[:])
            xt_ps[i] = ps

        def x_copy(i):
            s, tl = i // GT, i % GT
            dst = xg[s][:].rearrange("p k r e -> p (k r e)").bitcast(F32).rearrange("p (k r u) -> p k r u", k=KP, u=2)
            nc.scalar.copy(out=dst[:, :, tl * P : (tl + 1) * P, :], in_=xt_ps[i][:].rearrange("p k u r -> p k r u"))

        def x_turn(i):
            x_T(i)
            x_copy(i)

        def x_quant(s):
            xc[s] = xprep.tile([P, KP * NTOK], U32, name="xc", tag="xc", align_bytes=64)
            xs[s] = xprep.tile([P, KP * NTOK], U8, name="xs", tag="xs", align_bytes=64)
            nc.vector.quantize_mx(
                out=xc[s][:].bitcast(FP8X4), scales=xs[s][:], in_=xg[s][:].rearrange("p k r e -> p (k r e)")
            )

        def mm(s, jp):
            if jp == 0:
                hs[s] = hpool.tile([P, NJ, NTOK], F32, name="h", tag="h")
            acc = psum.tile([P, 2, NTOK], F32, name="acc", tag="acc")
            for jj in range(2):
                j = 2 * jp + jj
                cols = slice((j % 4) * P, (j % 4 + 1) * P)
                for kp in range(KP):
                    toks = slice(kp * NTOK, (kp + 1) * NTOK)
                    nc.tensor.matmul_mx(
                        out=acc[:, jj, :],
                        lhsT=wc[(kp, j // 4)][:, cols].bitcast(FP8X4),
                        lhsT_scale=ws[(kp, j // 4)][:, cols],
                        rhs=xc[s][:, toks].bitcast(FP8X4),
                        rhs_scale=xs[s][:, toks],
                        start=(kp == 0),
                        stop=(kp == KP - 1),
                    )
            for jj in range(2):
                j = 2 * jp + jj
                nc.scalar.activation(out=hs[s][:, j, :], in_=acc[:, jj, :], func=ACT.Silu, bias=b1f[:, j : j + 1], scale=1.0)

        def fold_T(i):
            s, tl = i // GT, i % GT
            toks = slice(tl * P, (tl + 1) * P)
            fold = psum.tile([P, P], F32, name="fold", tag="mu", bufs=1)
            for j in range(NJ):
                nc.tensor.matmul(
                    out=fold[:], lhsT=hs[s][:, j, toks], rhs=ident[:], is_transpose=True, start=(j == 0), stop=(j == NJ - 1)
                )
            fold_ps[i] = fold

        def fold_copy(i):
            gs[i] = stat.tile([P, 4], F32, name="gs", tag="gs")
            junk = stat.tile([P, HB], BF16, name="junk", tag="junk")
            nc.scalar.activation(out=junk[:, 0:P], in_=fold_ps[i][:], func=ACT.Copy, scale=-1.0 / H, accum_out=gs[i][:, 0:1])

        def h_T(i):
            s, tl = i // GT, i % GT
            toks = slice(tl * P, (tl + 1) * P)
            banks = []
            for half in range(2):
                ps = psum.tile([P, HB], F32, name="ht%d" % half, tag="ht%d" % half)
                for q in range(4):
                    nc.tensor.transpose(ps[:, q * P : (q + 1) * P], hs[s][:, 4 * half + q, toks], ident[:])
                banks.append(ps)
            ht_ps[i] = banks

        def v_stats(i):
            banks = ht_ps[i]
            gs[i] = stat.tile([P, 4], F32, name="gs", tag="gs")
            bn = stat.tile([P, 2, 6], F32, name="bn", tag="bn")
            for half in range(2):
                nc.vector.bn_stats(out=bn[:, half, :], in_=banks[half][:])
            mv = stat.tile([P, 2], F32, name="mv", tag="mv")
            nc.vector.bn_aggr(out=mv[:], in_=bn[:].rearrange("p a b -> p (a b)"))
            mean[i] = mv
            nc.gpsimd.tensor_scalar(
                out=gs[i][:, 1:2], in0=mv[:, 1:2], scalar1=float(H), scalar2=H * EPS_LN, op0=ALU.mult, op1=ALU.add
            )
            nc.gpsimd.tensor_tensor(out=gs[i][:, 2:3], in0=gs[i][:, 1:2], in1=mhalf[:], op=ALU.pow)

        def squares(i):
            banks = ht_ps[i]
            sp[i] = stat.tile([P, 2], F32, name="sp", tag="sp")
            for half in range(2):
                junk = stat.tile([P, HB], BF16, name="junk", tag="junk")
                nc.scalar.activation(
                    out=junk[:],
                    in_=banks[half][:],
                    func=ACT.Square,
                    bias=gs[i][:, 0:1],
                    scale=1.0,
                    accum_out=sp[i][:, half : half + 1],
                )
            nc.gpsimd.tensor_scalar(
                out=gs[i][:, 1:2], in0=sp[i][:, 0:1], scalar1=sp[i][:, 1:2], scalar2=H * EPS_LN, op0=ALU.add, op1=ALU.add
            )
            nc.gpsimd.tensor_tensor(out=gs[i][:, 2:3], in0=gs[i][:, 1:2], in1=mhalf[:], op=ALU.pow)

        zt = {}
        zT = {}
        oT = {}

        def p_norm(i):
            nc.scalar.activation(out=gs[i][:, 3:4], in_=gs[i][:, 0:1], func=ACT.Copy, scale=gs[i][:, 2:3])
            zt[i] = work.tile([P, H], F32, name="zt", tag="zt", bufs=1)
            for half in range(2):
                cols = slice(half * HB, (half + 1) * HB)
                nc.scalar.activation(
                    out=zt[i][:, cols], in_=ht_ps[i][half][:], func=ACT.Identity, scale=gs[i][:, 2:3], bias=gs[i][:, 3:4]
                )

        def p_back(i):
            zT[i] = []
            for half in range(2):
                ps = psum.tile([P, 4, P], F32, name="zT", tag="acc")
                for q in range(4):
                    j = 4 * half + q
                    nc.tensor.transpose(ps[:, q, :], zt[i][:, j * P : (j + 1) * P], ident[:])
                zT[i].append(ps)

        def p_affine(i):
            oT[i] = work.tile([P, H], F32, name="oT", tag="oT", bufs=1)
            for j in range(NJ):
                nc.scalar.activation(
                    out=oT[i][:, j * P : (j + 1) * P],
                    in_=zT[i][j // 4][:, j % 4, :],
                    func=ACT.Identity,
                    scale=g_col[:, j : j + 1],
                    bias=b1f[:, 2 * NJ + j : 2 * NJ + j + 1],
                )

        def p_out(i):
            s, tl = i // GT, i % GT
            if tl == 0:
                ob[s] = opool.tile([P, GT, H], F32, name="o", tag="o")
            for half in range(2):
                ps = psum.tile([P, HB], F32, name="ht%d" % half, tag="ht%d" % half)
                for q in range(4):
                    j = 4 * half + q
                    nc.tensor.transpose(ps[:, q * P : (q + 1) * P], oT[i][:, j * P : (j + 1) * P], ident[:])
                nc.scalar.copy(out=ob[s][:, tl, half * HB : (half + 1) * HB], in_=ps[:])

        def v1(i):
            tt[i] = work.tile([P, H], F32, name="t", tag="t")
            for half in range(2):
                cols = slice(half * HB, (half + 1) * HB)
                if i in mean:
                    nc.vector.scalar_tensor_tensor(
                        out=tt[i][:, cols], in0=ht_ps[i][half][:], scalar=mean[i][:, 0:1], in1=g_bc[:, cols], op0=ALU.subtract, op1=ALU.mult
                    )
                else:
                    nc.vector.scalar_tensor_tensor(
                        out=tt[i][:, cols], in0=ht_ps[i][half][:], scalar=gs[i][:, 0:1], in1=g_bc[:, cols], op0=ALU.add, op1=ALU.mult
                    )

        def v2(i):
            s, tl = i // GT, i % GT
            if tl == 0:
                ob[s] = opool.tile([P, GT, H], F32, name="o", tag="o")
            nc.vector.scalar_tensor_tensor(
                out=ob[s][:, tl, :], in0=tt[i][:], scalar=gs[i][:, 2:3], in1=beta_bc[:], op0=ALU.mult, op1=ALU.add
            )
            if tl == GT - 1:
                nc.sync.dma_start(out=o0_v[:, GT * s : GT * (s + 1), :], in_=ob[s][:])

        def v3(i):
            s, tl = i // GT, i % GT
            nc.vector.tensor_reduce(
                out=am[:, i : i + 1], in_=ob[s][:, tl, :], axis=AX.X, op=ALU.max, apply_absolute_value=True
            )

        def v_step(i):
            if 0 <= i < NT and i not in P_TILES:
                v1(i)
            if 0 <= i - 1 < NT and i - 1 not in P_TILES:
                v2(i - 1)
            if 0 <= i - 2 < NT and i - 2 not in P_TILES:
                v3(i - 2)

        x_turn(0)
        t0 = w_copy(0)
        x_turn(1)
        t1 = w_copy(1)
        spread_rows()
        w_quant(0, t0)
        x_quant(0)
        t2 = w_copy(2)
        w_quant(1, t1)
        t3 = w_copy(3)
        w_quant(2, t2)
        w_quant(3, t3)
        mm(0, 0)
        mm(0, 1)
        x_turn(2)
        mm(0, 2)
        mm(0, 3)
        x_turn(3)
        keep_rows()
        x_quant(1)
        for t in range(NT + 4):
            s, tl = t // GT, t % GT
            v_step(t - 2)
            if tl == 0 and 2 <= s + 1 < NG:
                x_quant(s + 1)
            if t == 0:
                for i in range(V_STAT_TILES):
                    h_T(i)
                    v_stats(i)
            has_x = t + 4 < NT
            has_h = V_STAT_TILES <= t < NT
            if has_x:
                x_T(t + 4)
            if has_h:
                fold_T(t)
                fold_copy(t)
            if has_x:
                x_copy(t + 4)
            if has_h:
                h_T(t)
                squares(t)
            if t - 1 in P_TILES:
                p_norm(t - 1)
                p_back(t - 1)
                p_affine(t - 1)
                p_out(t - 1)
            if s + 1 < NG:
                mm(s + 1, 2 * tl)
                mm(s + 1, 2 * tl + 1)

        for i in P_TILES:
            v3(i)

        gm = const.tile([P, 4], F32, name="gm")
        am_s = const.tile([P, NT], F32, name="am_s")
        nc.vector.tensor_scalar(
            out=am_s[:], in0=am[:], scalar1=1.0 / 448.0, scalar2=None, op0=ALU.mult, op1=ALU.max, accum_out=gm[:, 0:1]
        )
        spread = psum.tile([P, P], F32, name="spread", tag="xt", bufs=1)
        nc.tensor.transpose(spread[:], gm[:, 0:1].to_broadcast([P, P]), ident[:])
        nc.vector.tensor_reduce(out=gm[:, 1:2], in_=spread[:], axis=AX.X, op=ALU.max)
        nc.vector.reciprocal(out=gm[:, 3:4], in_=gm[:, 1:2])
        factor = gm[:, 3:4]

        for s in range(NG):
            flat = ob[s][:].rearrange("p a c -> p (a c)")
            f8 = opool.tile([P, GT * H], FP8, name="f8", tag="f8")
            nc.vector.tensor_scalar(
                out=f8[:, 0:CAST_V_COLS], in0=flat[:, 0:CAST_V_COLS], scalar1=factor, scalar2=None, op0=ALU.mult, saturate=False
            )
            nc.scalar.activation(
                out=f8[:, CAST_V_COLS:],
                in_=flat[:, CAST_V_COLS:],
                func=ACT.Identity,
                scale=factor,
                bias=zero[:, 0:1],
                saturate=False,
            )
            nc.sync.dma_start(out=o1_v[:, GT * H * s : GT * H * (s + 1)], in_=f8[:].bitcast(U8))
